import numpy as np
import ml_dtypes


def mxq(x, axis, fmt="e4m3"):
    dtype, down = {"e4m3": (ml_dtypes.float8_e4m3fn, 7), "e5m2": (ml_dtypes.float8_e5m2, 14)}[fmt]
    v = np.moveaxis(np.asarray(x, np.float32).astype(ml_dtypes.bfloat16).astype(np.float64), axis, -1)
    blocks = v.reshape(v.shape[:-1] + (-1, 32))
    amax = np.abs(blocks).max(-1, keepdims=True)
    byte = np.maximum(np.where(amax > 0, np.frexp(amax)[1] - 1 + 127, 0) - down, 1)
    scale = np.exp2(byte - 127.0)
    codes = (blocks / scale).astype(np.float32).astype(dtype).astype(np.float64)
    return np.moveaxis((codes * scale).reshape(v.shape), -1, axis)


WIDE = False


def mx_kscale(k):
    if not WIDE:
        return np.ones(k)
    levels = np.array([10, -10, 5, -5, 0])
    a = np.random.permutation(np.resize(levels, k // 512 * 4)).reshape(k // 512, 4)
    idx = np.arange(k)
    return np.exp2(a[idx // 512, idx % 128 // 32])


BF16 = ml_dtypes.bfloat16


def bf(x):
    return np.asarray(x, np.float32).astype(BF16)


def f64(x):
    return np.asarray(x).astype(np.float64)


E2M1 = np.array([0.0, 0.5, 1.0, 1.5, 2.0, 3.0, 4.0, 6.0, -0.0, -0.5, -1.0, -1.5, -2.0, -3.0, -4.0, -6.0])


def pack_weight(w, fmt):
    k, n = w.shape
    w = f64(bf(w)).reshape(k // 32, 32, n)
    amax = np.abs(w).max(1)
    if fmt == "e4m3":
        byte = np.frexp(amax)[1] - 1 + 127 - 7
    else:
        mant, ex = np.frexp(amax / 6.0)
        byte = np.where(mant > 0.5, ex, ex - 1) + 127
    byte = np.clip(np.where(amax > 0, byte, 1), 1, 254)
    scaled = (w * np.exp2(127.0 - byte)[:, None, :]).reshape(k, n).astype(np.float32)
    by_word = np.ascontiguousarray(scaled.reshape(k // 512, 128, 4, n).transpose(0, 1, 3, 2))
    if fmt == "e4m3":
        words = by_word.astype(ml_dtypes.float8_e4m3fn).view(np.uint8)
    else:
        c = by_word.astype(ml_dtypes.float4_e2m1fn).view(np.uint8) & 0xF
        words = c[..., 0::2] | (c[..., 1::2] << 4)
    return np.ascontiguousarray(words), np.ascontiguousarray(byte.astype(np.uint8).reshape(k // 512, 16, n))


def unpack_weight(words, scales, fmt):
    g, p, n, _ = words.shape
    if fmt == "e4m3":
        vals = np.ascontiguousarray(words).view(ml_dtypes.float8_e4m3fn).astype(np.float64)
    else:
        nib = np.empty((g, p, n, 4), np.uint8)
        nib[..., 0::2] = words & 0xF
        nib[..., 1::2] = words >> 4
        vals = E2M1[nib]
    vals = vals * np.repeat(np.exp2(scales.astype(np.float64) - 127.0), 8, axis=1)[..., None]
    return vals.transpose(0, 1, 3, 2).reshape(g * 512, n)

def pack4(w):
    words, scales = pack_weight(w, "e2m1")
    return words.reshape(words.shape[0], 128, -1), scales


def unpack4(words, scales):
    return unpack_weight(words.reshape(words.shape[0], 128, -1, 2), scales, "e2m1")


B, N, HID, H, D = 2, 4096, 1024, 1, 128


def apply_rope(t, rope):
    freqs = rope[:, 0, :]
    cos = np.repeat(freqs[:, 0::2], 2, axis=-1)[None, None]
    sin = np.repeat(freqs[:, 1::2], 2, axis=-1)[None, None]
    tr = t.reshape(*t.shape[:-1], -1, 2)
    t_real, t_imag = tr[..., 0], tr[..., 1]
    t_rot = np.stack([-t_imag, t_real], axis=-1).reshape(t.shape)
    return t * cos + t_rot * sin


def setup_inputs():
    s = mx_kscale(HID)
    x = bf(np.random.standard_normal((B, N, HID)) * s)
    rope = bf(np.random.uniform(size=(N, 1, D)))
    words, scales = pack4(np.random.standard_normal((HID, 3 * H * D)) * 1.5 / np.sqrt(HID) / s[:, None])
    return {"x": x,
            "rope": rope,
            "qkv_w_words": words,
            "qkv_w_scales": scales}


def reference(x, rope, qkv_w_words, qkv_w_scales):
    r = f64(rope)
    qkv = (mxq(f64(x), 2, "e4m3") @ unpack4(qkv_w_words, qkv_w_scales)).reshape(B, N, 3, H, D)
    q = np.transpose(qkv[:, :, 0], (0, 2, 1, 3))
    k = np.transpose(qkv[:, :, 1], (0, 2, 1, 3))
    v = np.transpose(qkv[:, :, 2], (0, 2, 1, 3))
    return apply_rope(q, r), apply_rope(k, r), v

@@ -1,0 +1,179 @@
+from contextlib import ExitStack
+
+import concourse.mybir as mybir
+from concourse.masks import make_identity
+
+F32 = mybir.dt.float32
+BF16 = mybir.dt.bfloat16
+I32 = mybir.dt.int32
+U32 = mybir.dt.uint32
+U8 = mybir.dt.uint8
+FP8X4 = mybir.dt.float8_e4m3fn_x4
+FP4X4 = mybir.dt.float4_e2m1fn_x4
+ALU = mybir.AluOpType
+
+BATCH, TOKENS, K, HEAD = 2, 4096, 1024, 128
+COMPONENTS = 3
+P = 128
+PACK = 4
+K_PASS = P * PACK
+PASSES = K // K_PASS
+TILES = 4
+CHUNK = P * TILES
+CHUNKS_PER_BATCH = TOKENS // CHUNK
+CHUNKS = BATCH * CHUNKS_PER_BATCH
+BANK = TILES * HEAD
+PAIRS = BANK // 2
+WORDS = K // 2
+X_BUFFERS = 6
+
+FLOPS = 2 * BATCH * TOKENS * K * COMPONENTS * HEAD
+
+
+def tile_attention_pa_t_kernel(tc, x, rope, qkv_w_words, qkv_w_scales, out_0, out_1, out_2):
+    nc = tc.nc
+
+    x_chunks = x.rearrange("b (c p t) k -> (b c) p (t k)", p=P, t=TILES)
+    rope_chunks = rope.rearrange("(c p t) o d -> c p (t o d)", p=P, t=TILES)
+    out_chunks = [
+        o.rearrange("b o (c p t) d -> (b o c) p (t d)", p=P, t=TILES) for o in (out_0, out_1, out_2)
+    ]
+
+    with ExitStack() as stack:
+        const = stack.enter_context(tc.tile_pool(name="const", bufs=1))
+        x_pool = stack.enter_context(tc.tile_pool(name="x", bufs=X_BUFFERS))
+        quant = stack.enter_context(tc.tile_pool(name="quant", bufs=2))
+        work = stack.enter_context(tc.tile_pool(name="work", bufs=3))
+        xt_pool = stack.enter_context(tc.psum_pool(name="xt", bufs=TILES))
+        acc_pool = stack.enter_context(tc.psum_pool(name="acc", bufs=4))
+
+        ident = const.tile([P, P], F32)
+        make_identity(nc, ident[:])
+
+        w_words = const.tile([P, PASSES * 2 * COMPONENTS * HEAD], U8, align_bytes=64)
+        w_scales = const.tile([P, PASSES * COMPONENTS * HEAD], U8, align_bytes=64)
+        nc.vector.memset(w_scales[:].bitcast(I32), 0)
+
+        rope_tiles = [const.tile([P, BANK], BF16, name="rope%d" % c) for c in range(CHUNKS_PER_BATCH)]
+        x_tiles = {}
+
+        def load(i):
+            x_sb = x_pool.tile([P, TILES * K], BF16)
+            nc.sync.dma_start(out=x_sb[:], in_=x_chunks[i])
+            x_tiles[i] = x_sb
+            if i < CHUNKS_PER_BATCH:
+                nc.sync.dma_start(out=rope_tiles[i][:], in_=rope_chunks[i])
+
+        def load_weights():
+            w_bytes = 2 * COMPONENTS * HEAD
+            w_cols = COMPONENTS * HEAD
+            for g in range(PASSES):
+                nc.sync.dma_start(
+                    out=w_words[:, g * w_bytes : (g + 1) * w_bytes].bitcast(I32),
+                    in_=qkv_w_words[g].bitcast(I32),
+                )
+            for g in range(PASSES):
+                for quadrant in range(4):
+                    nc.sync.dma_start(
+                        out=w_scales[32 * quadrant : 32 * quadrant + 4, g * w_cols : (g + 1) * w_cols].bitcast(I32),
+                        in_=qkv_w_scales[g, 4 * quadrant : 4 * quadrant + 4, :].bitcast(I32),
+                    )
+
+        grouped_tiles = {}
+        code_tiles = {}
+
+        def transpose(i):
+            words = x_tiles[i][:].bitcast(F32)
+            grouped = quant.tile([P, TILES * K], BF16, align_bytes=64)
+            grouped_words = grouped[:].bitcast(F32)
+            for t in range(TILES):
+                xt = xt_pool.tile([P, WORDS], F32)
+                for g in range(PASSES):
+                    for u in range(2):
+                        first = t * WORDS + g * 2 * P
+                        nc.tensor.transpose(
+                            xt[:, (2 * g + u) * P : (2 * g + u + 1) * P],
+                            words[:, first + u : first + 2 * P : 2],
+                            ident[:],
+                        )
+                nc.scalar.copy(
+                    out=grouped_words[:, t * WORDS : (t + 1) * WORDS].rearrange(
+                        "p (g r u) -> p g r u", g=PASSES, u=2
+                    ),
+                    in_=xt[:].rearrange("p (g u r) -> p g r u", g=PASSES, u=2),
+                )
+            grouped_tiles[i] = grouped
+
+        def quantise(i):
+            codes = quant.tile([P, TILES * PASSES * P], U32, align_bytes=64)
+            scales = quant.tile([P, TILES * PASSES * P], U8, align_bytes=64)
+            nc.vector.quantize_mx(out=codes[:].bitcast(FP8X4), scales=scales[:], in_=grouped_tiles[i][:])
+            code_tiles[i] = (codes, scales)
+
+        def project(i):
+            codes, scales = code_tiles[i]
+            banks = []
+            for c in range(COMPONENTS):
+                acc = acc_pool.tile([P, BANK], F32)
+                for t in range(TILES):
+                    for g in range(PASSES):
+                        tokens = slice((t * PASSES + g) * P, (t * PASSES + g + 1) * P)
+                        column = (g * COMPONENTS + c) * HEAD
+                        nc.tensor.matmul_mx(
+                            out=acc[:, t * HEAD : (t + 1) * HEAD],
+                            lhsT=codes[:, tokens].bitcast(FP8X4),
+                            lhsT_scale=scales[:, tokens],
+                            rhs=w_words[:, 2 * column : 2 * (column + HEAD)].bitcast(FP4X4),
+                            rhs_scale=w_scales[:, column : column + HEAD],
+                            start=(g == 0),
+                            stop=(g == PASSES - 1),
+                        )
+                banks.append(acc)
+            return banks
+
+        def rotate(acc, table, out_rows):
+            by_cos = work.tile([P, BANK], F32)
+            by_sin = work.tile([P, BANK], F32)
+            rotated = work.tile([P, BANK], F32)
+            pairs = "p (j e) -> p j e"
+            cos = table[:].rearrange(pairs, e=2)[:, :, 0:1].to_broadcast([P, PAIRS, 2])
+            sin = table[:, 1:BANK:2]
+            nc.vector.tensor_tensor(
+                out=by_cos[:].rearrange(pairs, e=2), in0=acc[:].rearrange(pairs, e=2), in1=cos, op=ALU.mult
+            )
+            nc.vector.scalar_tensor_tensor(
+                out=by_sin[:, 0:PAIRS], in0=acc[:, 1:BANK:2], scalar=-1.0, in1=sin, op0=ALU.mult, op1=ALU.mult
+            )
+            nc.vector.tensor_tensor(out=by_sin[:, PAIRS:BANK], in0=acc[:, 0:BANK:2], in1=sin, op=ALU.mult)
+            nc.gpsimd.tensor_tensor(
+                out=rotated[:].rearrange(pairs, e=2),
+                in0=by_cos[:].rearrange(pairs, e=2),
+                in1=by_sin[:].rearrange("p (e j) -> p j e", e=2),
+                op=ALU.add,
+            )
+            nc.sync.dma_start(out=out_rows, in_=rotated[:])
+
+        def finish(i, banks):
+            table = rope_tiles[i % CHUNKS_PER_BATCH]
+            rotate(banks[0], table, out_chunks[0][i])
+            rotate(banks[1], table, out_chunks[1][i])
+            v_sb = work.tile([P, BANK], F32)
+            nc.scalar.copy(out=v_sb[:], in_=banks[2][:])
+            nc.sync.dma_start(out=out_chunks[2][i], in_=v_sb[:])
+
+        with tc.manual_schedule():
+            load(0)
+            load_weights()
+            for i in range(1, X_BUFFERS):
+                load(i)
+            transpose(0)
+            quantise(0)
+            for i in range(CHUNKS):
+                if i + 1 < CHUNKS:
+                    transpose(i + 1)
+                banks = project(i)
+                if i + 1 < CHUNKS:
+                    quantise(i + 1)
+                finish(i, banks)
+                if i + X_BUFFERS < CHUNKS:
+                    load(i + X_BUFFERS)

@@ -25,7 +25,8 @@ CHUNKS = BATCH * CHUNKS_PER_BATCH
 BANK = TILES * HEAD
 PAIRS = BANK // 2
 WORDS = K // 2
-X_BUFFERS = 6
+X_BUFFERS = 8
+SORTED_TILES = 2
 
 FLOPS = 2 * BATCH * TOKENS * K * COMPONENTS * HEAD
 
@@ -57,45 +58,57 @@ def tile_attention_pa_t_kernel(tc, x, rope, qkv_w_words, qkv_w_scales, out_0, ou
         rope_tiles = [const.tile([P, BANK], BF16, name="rope%d" % c) for c in range(CHUNKS_PER_BATCH)]
         x_tiles = {}
 
-        def load(i):
+        def load(i, pieces=1):
             x_sb = x_pool.tile([P, TILES * K], BF16)
-            nc.sync.dma_start(out=x_sb[:], in_=x_chunks[i])
+            width = TILES * K // pieces
+            for piece in range(pieces):
+                columns = slice(piece * width, (piece + 1) * width)
+                nc.sync.dma_start(out=x_sb[:, columns], in_=x_chunks[i][:, columns])
             x_tiles[i] = x_sb
-            if i < CHUNKS_PER_BATCH:
-                nc.sync.dma_start(out=rope_tiles[i][:], in_=rope_chunks[i])
+
+        def load_rope(c):
+            nc.sync.dma_start(out=rope_tiles[c][:], in_=rope_chunks[c])
 
         def load_weights():
-            w_bytes = 2 * COMPONENTS * HEAD
-            w_cols = COMPONENTS * HEAD
-            for g in range(PASSES):
+            nc.sync.dma_start(
+                out=w_words[:].bitcast(I32).rearrange("p (g n) -> p g n", g=PASSES),
+                in_=qkv_w_words.bitcast(I32).rearrange("g p n -> p g n"),
+            )
+            for quadrant in range(4):
                 nc.sync.dma_start(
-                    out=w_words[:, g * w_bytes : (g + 1) * w_bytes].bitcast(I32),
-                    in_=qkv_w_words[g].bitcast(I32),
+                    out=w_scales[32 * quadrant : 32 * quadrant + 4, :].bitcast(I32).rearrange("r (g n) -> r g n", g=PASSES),
+                    in_=qkv_w_scales[:, 4 * quadrant : 4 * quadrant + 4, :].bitcast(I32).rearrange("g r n -> r g n"),
                 )
-            for g in range(PASSES):
-                for quadrant in range(4):
-                    nc.sync.dma_start(
-                        out=w_scales[32 * quadrant : 32 * quadrant + 4, g * w_cols : (g + 1) * w_cols].bitcast(I32),
-                        in_=qkv_w_scales[g, 4 * quadrant : 4 * quadrant + 4, :].bitcast(I32),
-                    )
 
+        sorted_tiles = {}
         grouped_tiles = {}
         code_tiles = {}
 
+        def sort(i):
+            words = x_tiles[i][:].bitcast(F32)[:, (TILES - SORTED_TILES) * WORDS :]
+            by_parity = quant.tile([P, SORTED_TILES * WORDS], F32)
+            nc.scalar.copy(
+                out=by_parity[:].rearrange("p (h u r) -> p h u r", u=2, r=P),
+                in_=words.rearrange("p (h r u) -> p h u r", u=2, r=P),
+            )
+            sorted_tiles[i] = by_parity
+
         def transpose(i):
             words = x_tiles[i][:].bitcast(F32)
+            by_parity = sorted_tiles[i]
             grouped = quant.tile([P, TILES * K], BF16, align_bytes=64)
             grouped_words = grouped[:].bitcast(F32)
             for t in range(TILES):
                 xt = xt_pool.tile([P, WORDS], F32)
                 for g in range(PASSES):
                     for u in range(2):
-                        first = t * WORDS + g * 2 * P
-                        nc.tensor.transpose(
-                            xt[:, (2 * g + u) * P : (2 * g + u + 1) * P],
-                            words[:, first + u : first + 2 * P : 2],
-                            ident[:],
-                        )
+                        if t < TILES - SORTED_TILES:
+                            first = t * WORDS + g * 2 * P
+                            columns = words[:, first + u : first + 2 * P : 2]
+                        else:
+                            first = (t - (TILES - SORTED_TILES)) * WORDS + (2 * g + u) * P
+                            columns = by_parity[:, first : first + P]
+                        nc.tensor.transpose(xt[:, (2 * g + u) * P : (2 * g + u + 1) * P], columns, ident[:])
                 nc.scalar.copy(
                     out=grouped_words[:, t * WORDS : (t + 1) * WORDS].rearrange(
                         "p (g r u) -> p g r u", g=PASSES, u=2
@@ -154,26 +167,35 @@ def tile_attention_pa_t_kernel(tc, x, rope, qkv_w_words, qkv_w_scales, out_0, ou
             nc.sync.dma_start(out=out_rows, in_=rotated[:])
 
         def finish(i, banks):
-            table = rope_tiles[i % CHUNKS_PER_BATCH]
-            rotate(banks[0], table, out_chunks[0][i])
-            rotate(banks[1], table, out_chunks[1][i])
             v_sb = work.tile([P, BANK], F32)
             nc.scalar.copy(out=v_sb[:], in_=banks[2][:])
             nc.sync.dma_start(out=out_chunks[2][i], in_=v_sb[:])
+            table = rope_tiles[i % CHUNKS_PER_BATCH]
+            rotate(banks[0], table, out_chunks[0][i])
+            rotate(banks[1], table, out_chunks[1][i])
 
         with tc.manual_schedule():
-            load(0)
+            load(0, pieces=TILES)
+            load(1)
             load_weights()
-            for i in range(1, X_BUFFERS):
+            load_rope(0)
+            for i in range(2, X_BUFFERS):
                 load(i)
+                load_rope(i - 1)
+            sort(0)
             transpose(0)
+            sort(1)
             quantise(0)
             for i in range(CHUNKS):
                 if i + 1 < CHUNKS:
                     transpose(i + 1)
+                if i + 2 < CHUNKS:
+                    sort(i + 2)
                 banks = project(i)
                 if i + 1 < CHUNKS:
                     quantise(i + 1)
                 finish(i, banks)
                 if i + X_BUFFERS < CHUNKS:
                     load(i + X_BUFFERS)
+                if i + X_BUFFERS - 1 < CHUNKS_PER_BATCH:
+                    load_rope(i + X_BUFFERS - 1)

@@ -25,8 +25,9 @@ CHUNKS = BATCH * CHUNKS_PER_BATCH
 BANK = TILES * HEAD
 PAIRS = BANK // 2
 WORDS = K // 2
-X_BUFFERS = 8
-SORTED_TILES = 2
+X_BUFFERS = 6
+OUT_CHUNKS = 5
+SORTED_TILES = 1
 
 FLOPS = 2 * BATCH * TOKENS * K * COMPONENTS * HEAD
 
@@ -44,7 +45,9 @@ def tile_attention_pa_t_kernel(tc, x, rope, qkv_w_words, qkv_w_scales, out_0, ou
         const = stack.enter_context(tc.tile_pool(name="const", bufs=1))
         x_pool = stack.enter_context(tc.tile_pool(name="x", bufs=X_BUFFERS))
         quant = stack.enter_context(tc.tile_pool(name="quant", bufs=2))
-        work = stack.enter_context(tc.tile_pool(name="work", bufs=3))
+        products = stack.enter_context(tc.tile_pool(name="products", bufs=3))
+        rotated_pool = stack.enter_context(tc.tile_pool(name="rotated", bufs=2 * OUT_CHUNKS))
+        v_pool = stack.enter_context(tc.tile_pool(name="v", bufs=OUT_CHUNKS))
         xt_pool = stack.enter_context(tc.psum_pool(name="xt", bufs=TILES))
         acc_pool = stack.enter_context(tc.psum_pool(name="acc", bufs=4))
 
@@ -120,7 +123,13 @@ def tile_attention_pa_t_kernel(tc, x, rope, qkv_w_words, qkv_w_scales, out_0, ou
         def quantise(i):
             codes = quant.tile([P, TILES * PASSES * P], U32, align_bytes=64)
             scales = quant.tile([P, TILES * PASSES * P], U8, align_bytes=64)
-            nc.vector.quantize_mx(out=codes[:].bitcast(FP8X4), scales=scales[:], in_=grouped_tiles[i][:])
+            for t in range(TILES):
+                columns = slice(t * PASSES * P, (t + 1) * PASSES * P)
+                nc.vector.quantize_mx(
+                    out=codes[:, columns].bitcast(FP8X4),
+                    scales=scales[:, columns],
+                    in_=grouped_tiles[i][:, t * K : (t + 1) * K],
+                )
             code_tiles[i] = (codes, scales)
 
         def project(i):
@@ -145,9 +154,9 @@ def tile_attention_pa_t_kernel(tc, x, rope, qkv_w_words, qkv_w_scales, out_0, ou
             return banks
 
         def rotate(acc, table, out_rows):
-            by_cos = work.tile([P, BANK], F32)
-            by_sin = work.tile([P, BANK], F32)
-            rotated = work.tile([P, BANK], F32)
+            by_cos = products.tile([P, BANK], F32)
+            by_sin = products.tile([P, BANK], F32)
+            rotated = rotated_pool.tile([P, BANK], F32)
             pairs = "p (j e) -> p j e"
             cos = table[:].rearrange(pairs, e=2)[:, :, 0:1].to_broadcast([P, PAIRS, 2])
             sin = table[:, 1:BANK:2]
@@ -167,7 +176,7 @@ def tile_attention_pa_t_kernel(tc, x, rope, qkv_w_words, qkv_w_scales, out_0, ou
             nc.sync.dma_start(out=out_rows, in_=rotated[:])
 
         def finish(i, banks):
-            v_sb = work.tile([P, BANK], F32)
+            v_sb = v_pool.tile([P, BANK], F32)
             nc.scalar.copy(out=v_sb[:], in_=banks[2][:])
             nc.sync.dma_start(out=out_chunks[2][i], in_=v_sb[:])
             table = rope_tiles[i % CHUNKS_PER_BATCH]

@@ -27,6 +27,7 @@ PAIRS = BANK // 2
 WORDS = K // 2
 X_BUFFERS = 6
 OUT_CHUNKS = 5
+PROJECT_ORDER = (2, 0, 1)
 SORTED_TILES = 1
 
 FLOPS = 2 * BATCH * TOKENS * K * COMPONENTS * HEAD
@@ -134,8 +135,8 @@ def tile_attention_pa_t_kernel(tc, x, rope, qkv_w_words, qkv_w_scales, out_0, ou
 
         def project(i):
             codes, scales = code_tiles[i]
-            banks = []
-            for c in range(COMPONENTS):
+            banks = {}
+            for c in PROJECT_ORDER:
                 acc = acc_pool.tile([P, BANK], F32)
                 for t in range(TILES):
                     for g in range(PASSES):
@@ -150,23 +151,27 @@ def tile_attention_pa_t_kernel(tc, x, rope, qkv_w_words, qkv_w_scales, out_0, ou
                             start=(g == 0),
                             stop=(g == PASSES - 1),
                         )
-                banks.append(acc)
+                banks[c] = acc
             return banks
 
-        def rotate(acc, table, out_rows):
+        pairs = "p (j e) -> p j e"
+
+        def rotate_early(acc, table):
             by_cos = products.tile([P, BANK], F32)
             by_sin = products.tile([P, BANK], F32)
-            rotated = rotated_pool.tile([P, BANK], F32)
-            pairs = "p (j e) -> p j e"
             cos = table[:].rearrange(pairs, e=2)[:, :, 0:1].to_broadcast([P, PAIRS, 2])
-            sin = table[:, 1:BANK:2]
             nc.vector.tensor_tensor(
                 out=by_cos[:].rearrange(pairs, e=2), in0=acc[:].rearrange(pairs, e=2), in1=cos, op=ALU.mult
             )
             nc.vector.scalar_tensor_tensor(
-                out=by_sin[:, 0:PAIRS], in0=acc[:, 1:BANK:2], scalar=-1.0, in1=sin, op0=ALU.mult, op1=ALU.mult
+                out=by_sin[:, 0:PAIRS], in0=acc[:, 1:BANK:2], scalar=-1.0, in1=table[:, 1:BANK:2],
+                op0=ALU.mult, op1=ALU.mult,
             )
-            nc.vector.tensor_tensor(out=by_sin[:, PAIRS:BANK], in0=acc[:, 0:BANK:2], in1=sin, op=ALU.mult)
+            return by_cos, by_sin
+
+        def rotate_late(acc, table, by_cos, by_sin, out_rows):
+            rotated = rotated_pool.tile([P, BANK], F32)
+            nc.vector.tensor_tensor(out=by_sin[:, PAIRS:BANK], in0=acc[:, 0:BANK:2], in1=table[:, 1:BANK:2], op=ALU.mult)
             nc.gpsimd.tensor_tensor(
                 out=rotated[:].rearrange(pairs, e=2),
                 in0=by_cos[:].rearrange(pairs, e=2),
@@ -175,13 +180,23 @@ def tile_attention_pa_t_kernel(tc, x, rope, qkv_w_words, qkv_w_scales, out_0, ou
             )
             nc.sync.dma_start(out=out_rows, in_=rotated[:])
 
+        held = {}
+
+        def finish_k(i):
+            acc, table, by_cos, by_sin = held[i]
+            rotate_late(acc, table, by_cos, by_sin, out_chunks[1][i])
+
         def finish(i, banks):
             v_sb = v_pool.tile([P, BANK], F32)
             nc.scalar.copy(out=v_sb[:], in_=banks[2][:])
             nc.sync.dma_start(out=out_chunks[2][i], in_=v_sb[:])
+            if i > 0:
+                finish_k(i - 1)
             table = rope_tiles[i % CHUNKS_PER_BATCH]
-            rotate(banks[0], table, out_chunks[0][i])
-            rotate(banks[1], table, out_chunks[1][i])
+            by_cos, by_sin = rotate_early(banks[0], table)
+            rotate_late(banks[0], table, by_cos, by_sin, out_chunks[0][i])
+            by_cos, by_sin = rotate_early(banks[1], table)
+            held[i] = (banks[1], table, by_cos, by_sin)
 
         with tc.manual_schedule():
             load(0, pieces=TILES)
@@ -208,3 +223,4 @@ def tile_attention_pa_t_kernel(tc, x, rope, qkv_w_words, qkv_w_scales, out_0, ou
                     load(i + X_BUFFERS)
                 if i + X_BUFFERS - 1 < CHUNKS_PER_BATCH:
                     load_rope(i + X_BUFFERS - 1)
+            finish_k(CHUNKS - 1)

@@ -169,10 +169,12 @@ def tile_attention_pa_t_kernel(tc, x, rope, qkv_w_words, qkv_w_scales, out_0, ou
             )
             return by_cos, by_sin
 
-        def rotate_late(acc, table, by_cos, by_sin, out_rows):
-            rotated = rotated_pool.tile([P, BANK], F32)
+        def third_product(acc, table, by_sin):
             nc.vector.tensor_tensor(out=by_sin[:, PAIRS:BANK], in0=acc[:, 0:BANK:2], in1=table[:, 1:BANK:2], op=ALU.mult)
-            nc.gpsimd.tensor_tensor(
+
+        def add_and_store(engine, by_cos, by_sin, out_rows):
+            rotated = rotated_pool.tile([P, BANK], F32)
+            engine.tensor_tensor(
                 out=rotated[:].rearrange(pairs, e=2),
                 in0=by_cos[:].rearrange(pairs, e=2),
                 in1=by_sin[:].rearrange("p (e j) -> p j e", e=2),
@@ -182,21 +184,23 @@ def tile_attention_pa_t_kernel(tc, x, rope, qkv_w_words, qkv_w_scales, out_0, ou
 
         held = {}
 
-        def finish_k(i):
+        def finish_k(i, engine):
             acc, table, by_cos, by_sin = held[i]
-            rotate_late(acc, table, by_cos, by_sin, out_chunks[1][i])
+            third_product(acc, table, by_sin)
+            add_and_store(engine, by_cos, by_sin, out_chunks[1][i])
 
         def finish(i, banks):
             v_sb = v_pool.tile([P, BANK], F32)
             nc.scalar.copy(out=v_sb[:], in_=banks[2][:])
             nc.sync.dma_start(out=out_chunks[2][i], in_=v_sb[:])
             if i > 0:
-                finish_k(i - 1)
+                finish_k(i - 1, nc.gpsimd)
             table = rope_tiles[i % CHUNKS_PER_BATCH]
-            by_cos, by_sin = rotate_early(banks[0], table)
-            rotate_late(banks[0], table, by_cos, by_sin, out_chunks[0][i])
-            by_cos, by_sin = rotate_early(banks[1], table)
-            held[i] = (banks[1], table, by_cos, by_sin)
+            q_cos, q_sin = rotate_early(banks[0], table)
+            third_product(banks[0], table, q_sin)
+            k_cos, k_sin = rotate_early(banks[1], table)
+            held[i] = (banks[1], table, k_cos, k_sin)
+            add_and_store(nc.vector, q_cos, q_sin, out_chunks[0][i])
 
         with tc.manual_schedule():
             load(0, pieces=TILES)
@@ -223,4 +227,4 @@ def tile_attention_pa_t_kernel(tc, x, rope, qkv_w_words, qkv_w_scales, out_0, ou
                     load(i + X_BUFFERS)
                 if i + X_BUFFERS - 1 < CHUNKS_PER_BATCH:
                     load_rope(i + X_BUFFERS - 1)
-            finish_k(CHUNKS - 1)
+            finish_k(CHUNKS - 1, nc.vector)

@@ -28,6 +28,7 @@ WORDS = K // 2
 X_BUFFERS = 6
 OUT_CHUNKS = 5
 PROJECT_ORDER = (2, 0, 1)
+VECTOR_SUMS = 3
 SORTED_TILES = 1
 
 FLOPS = 2 * BATCH * TOKENS * K * COMPONENTS * HEAD
@@ -47,7 +48,7 @@ def tile_attention_pa_t_kernel(tc, x, rope, qkv_w_words, qkv_w_scales, out_0, ou
         x_pool = stack.enter_context(tc.tile_pool(name="x", bufs=X_BUFFERS))
         quant = stack.enter_context(tc.tile_pool(name="quant", bufs=2))
         products = stack.enter_context(tc.tile_pool(name="products", bufs=3))
-        rotated_pool = stack.enter_context(tc.tile_pool(name="rotated", bufs=2 * OUT_CHUNKS))
+        rotated_pool = stack.enter_context(tc.tile_pool(name="rotated", bufs=OUT_CHUNKS + 1))
         v_pool = stack.enter_context(tc.tile_pool(name="v", bufs=OUT_CHUNKS))
         xt_pool = stack.enter_context(tc.psum_pool(name="xt", bufs=TILES))
         acc_pool = stack.enter_context(tc.psum_pool(name="acc", bufs=4))
@@ -155,52 +156,69 @@ def tile_attention_pa_t_kernel(tc, x, rope, qkv_w_words, qkv_w_scales, out_0, ou
             return banks
 
         pairs = "p (j e) -> p j e"
+        HALF = HEAD // 2
 
-        def rotate_early(acc, table):
-            by_cos = products.tile([P, BANK], F32)
-            by_sin = products.tile([P, BANK], F32)
+        def factor(table, e):
+            return table[:].rearrange("p (t j e) -> p e t j", t=TILES, e=2)[:, e]
+
+        def start_rope(i):
+            by_cos = products.tile([P, 2 * BANK], F32)
+            by_sin = products.tile([P, 2 * BANK], F32)
+            rotated = rotated_pool.tile([P, 2 * BANK], F32)
+            return by_cos, by_sin, rotated
+
+        def cos_product(acc, table, by_cos, c):
             cos = table[:].rearrange(pairs, e=2)[:, :, 0:1].to_broadcast([P, PAIRS, 2])
             nc.vector.tensor_tensor(
-                out=by_cos[:].rearrange(pairs, e=2), in0=acc[:].rearrange(pairs, e=2), in1=cos, op=ALU.mult
+                out=by_cos[:, c * BANK : (c + 1) * BANK].rearrange(pairs, e=2),
+                in0=acc[:].rearrange(pairs, e=2),
+                in1=cos,
+                op=ALU.mult,
             )
-            nc.vector.scalar_tensor_tensor(
-                out=by_sin[:, 0:PAIRS], in0=acc[:, 1:BANK:2], scalar=-1.0, in1=table[:, 1:BANK:2],
-                op0=ALU.mult, op1=ALU.mult,
-            )
-            return by_cos, by_sin
 
-        def third_product(acc, table, by_sin):
-            nc.vector.tensor_tensor(out=by_sin[:, PAIRS:BANK], in0=acc[:, 0:BANK:2], in1=table[:, 1:BANK:2], op=ALU.mult)
+        def sin_product(acc, table, by_sin, c, e):
+            out = by_sin[:, c * BANK : (c + 1) * BANK].rearrange("p (t e j) -> p e t j", t=TILES, e=2)[:, e]
+            other = acc[:].rearrange("p (t j e) -> p e t j", t=TILES, e=2)[:, 1 - e]
+            if e == 0:
+                nc.vector.scalar_tensor_tensor(
+                    out=out, in0=other, scalar=-1.0, in1=factor(table, 1), op0=ALU.mult, op1=ALU.mult
+                )
+            else:
+                nc.vector.tensor_tensor(out=out, in0=other, in1=factor(table, 1), op=ALU.mult)
 
-        def add_and_store(engine, by_cos, by_sin, out_rows):
-            rotated = rotated_pool.tile([P, BANK], F32)
+        def add(engine, by_cos, by_sin, rotated, first, last):
+            columns = slice(first * HEAD, last * HEAD)
             engine.tensor_tensor(
-                out=rotated[:].rearrange(pairs, e=2),
-                in0=by_cos[:].rearrange(pairs, e=2),
-                in1=by_sin[:].rearrange("p (e j) -> p j e", e=2),
+                out=rotated[:, columns].rearrange("p (t j e) -> p t j e", j=HALF, e=2),
+                in0=by_cos[:, columns].rearrange("p (t j e) -> p t j e", j=HALF, e=2),
+                in1=by_sin[:, columns].rearrange("p (t e j) -> p t j e", j=HALF, e=2),
                 op=ALU.add,
             )
-            nc.sync.dma_start(out=out_rows, in_=rotated[:])
 
         held = {}
 
-        def finish_k(i, engine):
-            acc, table, by_cos, by_sin = held[i]
-            third_product(acc, table, by_sin)
-            add_and_store(engine, by_cos, by_sin, out_chunks[1][i])
+        def finish_late(i, engine):
+            acc, table, by_cos, by_sin, rotated = held[i]
+            sin_product(acc, table, by_sin, 1, 1)
+            add(engine, by_cos, by_sin, rotated, VECTOR_SUMS, 2 * TILES)
+            nc.sync.dma_start(out=out_chunks[0][i], in_=rotated[:, 0:BANK])
+            nc.sync.dma_start(out=out_chunks[1][i], in_=rotated[:, BANK : 2 * BANK])
 
         def finish(i, banks):
             v_sb = v_pool.tile([P, BANK], F32)
             nc.scalar.copy(out=v_sb[:], in_=banks[2][:])
             nc.sync.dma_start(out=out_chunks[2][i], in_=v_sb[:])
             if i > 0:
-                finish_k(i - 1, nc.gpsimd)
+                finish_late(i - 1, nc.gpsimd)
             table = rope_tiles[i % CHUNKS_PER_BATCH]
-            q_cos, q_sin = rotate_early(banks[0], table)
-            third_product(banks[0], table, q_sin)
-            k_cos, k_sin = rotate_early(banks[1], table)
-            held[i] = (banks[1], table, k_cos, k_sin)
-            add_and_store(nc.vector, q_cos, q_sin, out_chunks[0][i])
+            by_cos, by_sin, rotated = start_rope(i)
+            cos_product(banks[0], table, by_cos, 0)
+            sin_product(banks[0], table, by_sin, 0, 0)
+            sin_product(banks[0], table, by_sin, 0, 1)
+            cos_product(banks[1], table, by_cos, 1)
+            sin_product(banks[1], table, by_sin, 1, 0)
+            held[i] = (banks[1], table, by_cos, by_sin, rotated)
+            add(nc.vector, by_cos, by_sin, rotated, 0, VECTOR_SUMS)
 
         with tc.manual_schedule():
             load(0, pieces=TILES)
@@ -227,4 +245,4 @@ def tile_attention_pa_t_kernel(tc, x, rope, qkv_w_words, qkv_w_scales, out_0, ou
                     load(i + X_BUFFERS)
                 if i + X_BUFFERS - 1 < CHUNKS_PER_BATCH:
                     load_rope(i + X_BUFFERS - 1)
-            finish_k(CHUNKS - 1, nc.vector)
+            finish_late(CHUNKS - 1, nc.vector)

@@ -122,11 +122,13 @@ def tile_attention_pa_t_kernel(tc, x, rope, qkv_w_words, qkv_w_scales, out_0, ou
                 )
             grouped_tiles[i] = grouped
 
-        def quantise(i):
+        def quantise(i, before_last=None):
             codes = quant.tile([P, TILES * PASSES * P], U32, align_bytes=64)
             scales = quant.tile([P, TILES * PASSES * P], U8, align_bytes=64)
             for t in range(TILES):
                 columns = slice(t * PASSES * P, (t + 1) * PASSES * P)
+                if t == TILES - 1 and before_last is not None:
+                    before_last()
                 nc.vector.quantize_mx(
                     out=codes[:, columns].bitcast(FP8X4),
                     scales=scales[:, columns],
@@ -196,6 +198,7 @@ def tile_attention_pa_t_kernel(tc, x, rope, qkv_w_words, qkv_w_scales, out_0, ou
             )
 
         held = {}
+        late = {}
 
         def finish_late(i, engine):
             acc, table, by_cos, by_sin, rotated = held[i]
@@ -204,12 +207,12 @@ def tile_attention_pa_t_kernel(tc, x, rope, qkv_w_words, qkv_w_scales, out_0, ou
             nc.sync.dma_start(out=out_chunks[0][i], in_=rotated[:, 0:BANK])
             nc.sync.dma_start(out=out_chunks[1][i], in_=rotated[:, BANK : 2 * BANK])
 
-        def finish(i, banks):
+        def finish_v(i, banks):
             v_sb = v_pool.tile([P, BANK], F32)
             nc.scalar.copy(out=v_sb[:], in_=banks[2][:])
             nc.sync.dma_start(out=out_chunks[2][i], in_=v_sb[:])
-            if i > 0:
-                finish_late(i - 1, nc.gpsimd)
+
+        def finish(i, banks):
             table = rope_tiles[i % CHUNKS_PER_BATCH]
             by_cos, by_sin, rotated = start_rope(i)
             cos_product(banks[0], table, by_cos, 0)
@@ -218,6 +221,7 @@ def tile_attention_pa_t_kernel(tc, x, rope, qkv_w_words, qkv_w_scales, out_0, ou
             cos_product(banks[1], table, by_cos, 1)
             sin_product(banks[1], table, by_sin, 1, 0)
             held[i] = (banks[1], table, by_cos, by_sin, rotated)
+            late[i] = lambda: finish_late(i, nc.gpsimd)
             add(nc.vector, by_cos, by_sin, rotated, 0, VECTOR_SUMS)
 
         with tc.manual_schedule():
@@ -238,8 +242,13 @@ def tile_attention_pa_t_kernel(tc, x, rope, qkv_w_words, qkv_w_scales, out_0, ou
                 if i + 2 < CHUNKS:
                     sort(i + 2)
                 banks = project(i)
-                if i + 1 < CHUNKS:
-                    quantise(i + 1)
+                finish_v(i, banks)
+                if i == 0:
+                    quantise(1)
+                elif i + 1 < CHUNKS:
+                    quantise(i + 1, before_last=late[i - 1])
+                else:
+                    late[i - 1]()
                 finish(i, banks)
                 if i + X_BUFFERS < CHUNKS:
                     load(i + X_BUFFERS)

@@ -100,18 +100,19 @@ def tile_attention_pa_t_kernel(tc, x, rope, qkv_w_words, qkv_w_scales, out_0, ou
 
         def transpose(i):
             words = x_tiles[i][:].bitcast(F32)
-            by_parity = sorted_tiles[i]
+            by_parity = sorted_tiles.get(i)
+            unsorted = TILES if by_parity is None else TILES - SORTED_TILES
             grouped = quant.tile([P, TILES * K], BF16, align_bytes=64)
             grouped_words = grouped[:].bitcast(F32)
             for t in range(TILES):
                 xt = xt_pool.tile([P, WORDS], F32)
                 for g in range(PASSES):
                     for u in range(2):
-                        if t < TILES - SORTED_TILES:
+                        if t < unsorted:
                             first = t * WORDS + g * 2 * P
                             columns = words[:, first + u : first + 2 * P : 2]
                         else:
-                            first = (t - (TILES - SORTED_TILES)) * WORDS + (2 * g + u) * P
+                            first = (t - unsorted) * WORDS + (2 * g + u) * P
                             columns = by_parity[:, first : first + P]
                         nc.tensor.transpose(xt[:, (2 * g + u) * P : (2 * g + u + 1) * P], columns, ident[:])
                 nc.scalar.copy(
@@ -207,6 +208,16 @@ def tile_attention_pa_t_kernel(tc, x, rope, qkv_w_words, qkv_w_scales, out_0, ou
             nc.sync.dma_start(out=out_chunks[0][i], in_=rotated[:, 0:BANK])
             nc.sync.dma_start(out=out_chunks[1][i], in_=rotated[:, BANK : 2 * BANK])
 
+        def finish_last(i):
+            acc, table, by_cos, by_sin, rotated = held[i]
+            sin_product(acc, table, by_sin, 1, 1)
+            for first in (TILES, TILES + TILES // 2):
+                add(nc.vector, by_cos, by_sin, rotated, first, first + TILES // 2)
+                columns = slice((first - TILES) * HEAD, (first - TILES // 2) * HEAD)
+                nc.sync.dma_start(
+                    out=out_chunks[1][i][:, columns], in_=rotated[:, first * HEAD : (first + TILES // 2) * HEAD]
+                )
+
         def finish_v(i, banks):
             v_sb = v_pool.tile([P, BANK], F32)
             nc.scalar.copy(out=v_sb[:], in_=banks[2][:])
@@ -222,19 +233,21 @@ def tile_attention_pa_t_kernel(tc, x, rope, qkv_w_words, qkv_w_scales, out_0, ou
             sin_product(banks[1], table, by_sin, 1, 0)
             held[i] = (banks[1], table, by_cos, by_sin, rotated)
             late[i] = lambda: finish_late(i, nc.gpsimd)
-            add(nc.vector, by_cos, by_sin, rotated, 0, VECTOR_SUMS)
+            if i < CHUNKS - 1:
+                add(nc.vector, by_cos, by_sin, rotated, 0, VECTOR_SUMS)
+            else:
+                add(nc.vector, by_cos, by_sin, rotated, 0, TILES)
+                nc.sync.dma_start(out=out_chunks[0][i], in_=rotated[:, 0:BANK])
 
         with tc.manual_schedule():
             load(0, pieces=TILES)
-            load(1)
+            load(1, pieces=TILES)
             load_weights()
             load_rope(0)
             for i in range(2, X_BUFFERS):
                 load(i)
                 load_rope(i - 1)
-            sort(0)
             transpose(0)
-            sort(1)
             quantise(0)
             for i in range(CHUNKS):
                 if i + 1 < CHUNKS:
@@ -254,4 +267,4 @@ def tile_attention_pa_t_kernel(tc, x, rope, qkv_w_words, qkv_w_scales, out_0, ou
                     load(i + X_BUFFERS)
                 if i + X_BUFFERS - 1 < CHUNKS_PER_BATCH:
                     load_rope(i + X_BUFFERS - 1)
-            finish_late(CHUNKS - 1, nc.vector)
+            finish_last(CHUNKS - 1)

@@ -161,8 +161,6 @@ def tile_attention_pa_t_kernel(tc, x, rope, qkv_w_words, qkv_w_scales, out_0, ou
         pairs = "p (j e) -> p j e"
         HALF = HEAD // 2
 
-        def factor(table, e):
-            return table[:].rearrange("p (t j e) -> p e t j", t=TILES, e=2)[:, e]
 
         def start_rope(i):
             by_cos = products.tile([P, 2 * BANK], F32)
@@ -179,15 +177,14 @@ def tile_attention_pa_t_kernel(tc, x, rope, qkv_w_words, qkv_w_scales, out_0, ou
                 op=ALU.mult,
             )
 
-        def sin_product(acc, table, by_sin, c, e):
-            out = by_sin[:, c * BANK : (c + 1) * BANK].rearrange("p (t e j) -> p e t j", t=TILES, e=2)[:, e]
-            other = acc[:].rearrange("p (t j e) -> p e t j", t=TILES, e=2)[:, 1 - e]
+        def sin_product(acc, table, by_sin, c, e, first=0, last=TILES):
+            out = by_sin[:, c * BANK : (c + 1) * BANK].rearrange("p (t e j) -> p e t j", t=TILES, e=2)[:, e, first:last, :]
+            other = acc[:].rearrange("p (t j e) -> p e t j", t=TILES, e=2)[:, 1 - e, first:last, :]
+            sin = table[:].rearrange("p (t j e) -> p e t j", t=TILES, e=2)[:, 1, first:last, :]
             if e == 0:
-                nc.vector.scalar_tensor_tensor(
-                    out=out, in0=other, scalar=-1.0, in1=factor(table, 1), op0=ALU.mult, op1=ALU.mult
-                )
+                nc.vector.scalar_tensor_tensor(out=out, in0=other, scalar=-1.0, in1=sin, op0=ALU.mult, op1=ALU.mult)
             else:
-                nc.vector.tensor_tensor(out=out, in0=other, in1=factor(table, 1), op=ALU.mult)
+                nc.vector.tensor_tensor(out=out, in0=other, in1=sin, op=ALU.mult)
 
         def add(engine, by_cos, by_sin, rotated, first, last):
             columns = slice(first * HEAD, last * HEAD)
@@ -203,14 +200,14 @@ def tile_attention_pa_t_kernel(tc, x, rope, qkv_w_words, qkv_w_scales, out_0, ou
 
         def finish_late(i, engine):
             acc, table, by_cos, by_sin, rotated = held[i]
-            sin_product(acc, table, by_sin, 1, 1)
+            sin_product(acc, table, by_sin, 1, 1, TILES - 1, TILES)
             add(engine, by_cos, by_sin, rotated, VECTOR_SUMS, 2 * TILES)
             nc.sync.dma_start(out=out_chunks[0][i], in_=rotated[:, 0:BANK])
             nc.sync.dma_start(out=out_chunks[1][i], in_=rotated[:, BANK : 2 * BANK])
 
         def finish_last(i):
             acc, table, by_cos, by_sin, rotated = held[i]
-            sin_product(acc, table, by_sin, 1, 1)
+            sin_product(acc, table, by_sin, 1, 1, TILES - 1, TILES)
             for first in (TILES, TILES + TILES // 2):
                 add(nc.vector, by_cos, by_sin, rotated, first, first + TILES // 2)
                 columns = slice((first - TILES) * HEAD, (first - TILES // 2) * HEAD)
@@ -231,6 +228,7 @@ def tile_attention_pa_t_kernel(tc, x, rope, qkv_w_words, qkv_w_scales, out_0, ou
             sin_product(banks[0], table, by_sin, 0, 1)
             cos_product(banks[1], table, by_cos, 1)
             sin_product(banks[1], table, by_sin, 1, 0)
+            sin_product(banks[1], table, by_sin, 1, 1, 0, TILES - 1)
             held[i] = (banks[1], table, by_cos, by_sin, rotated)
             late[i] = lambda: finish_late(i, nc.gpsimd)
             if i < CHUNKS - 1:

@@ -29,6 +29,7 @@ X_BUFFERS = 6
 OUT_CHUNKS = 5
 PROJECT_ORDER = (2, 0, 1)
 VECTOR_SUMS = 3
+LATE_V = (4, 9)
 SORTED_TILES = 1
 
 FLOPS = 2 * BATCH * TOKENS * K * COMPONENTS * HEAD
@@ -47,6 +48,7 @@ def tile_attention_pa_t_kernel(tc, x, rope, qkv_w_words, qkv_w_scales, out_0, ou
         const = stack.enter_context(tc.tile_pool(name="const", bufs=1))
         x_pool = stack.enter_context(tc.tile_pool(name="x", bufs=X_BUFFERS))
         quant = stack.enter_context(tc.tile_pool(name="quant", bufs=2))
+        kept_pool = stack.enter_context(tc.tile_pool(name="kept", bufs=len(LATE_V)))
         products = stack.enter_context(tc.tile_pool(name="products", bufs=3))
         rotated_pool = stack.enter_context(tc.tile_pool(name="rotated", bufs=OUT_CHUNKS + 1))
         v_pool = stack.enter_context(tc.tile_pool(name="v", bufs=OUT_CHUNKS))
@@ -105,7 +107,7 @@ def tile_attention_pa_t_kernel(tc, x, rope, qkv_w_words, qkv_w_scales, out_0, ou
             grouped = quant.tile([P, TILES * K], BF16, align_bytes=64)
             grouped_words = grouped[:].bitcast(F32)
             for t in range(TILES):
-                xt = xt_pool.tile([P, WORDS], F32)
+                xt = xt_pool.tile([P, WORDS], F32, name="xt")
                 for g in range(PASSES):
                     for u in range(2):
                         if t < unsorted:
@@ -124,8 +126,9 @@ def tile_attention_pa_t_kernel(tc, x, rope, qkv_w_words, qkv_w_scales, out_0, ou
             grouped_tiles[i] = grouped
 
         def quantise(i, before_last=None):
-            codes = quant.tile([P, TILES * PASSES * P], U32, align_bytes=64)
-            scales = quant.tile([P, TILES * PASSES * P], U8, align_bytes=64)
+            pool = kept_pool if i in LATE_V else quant
+            codes = pool.tile([P, TILES * PASSES * P], U32, align_bytes=64)
+            scales = pool.tile([P, TILES * PASSES * P], U8, align_bytes=64)
             for t in range(TILES):
                 columns = slice(t * PASSES * P, (t + 1) * PASSES * P)
                 if t == TILES - 1 and before_last is not None:
@@ -137,11 +140,11 @@ def tile_attention_pa_t_kernel(tc, x, rope, qkv_w_words, qkv_w_scales, out_0, ou
                 )
             code_tiles[i] = (codes, scales)
 
-        def project(i):
+        def project(i, components, pool, tag):
             codes, scales = code_tiles[i]
             banks = {}
-            for c in PROJECT_ORDER:
-                acc = acc_pool.tile([P, BANK], F32)
+            for c in components:
+                acc = pool.tile([P, BANK], F32, name=tag)
                 for t in range(TILES):
                     for g in range(PASSES):
                         tokens = slice((t * PASSES + g) * P, (t * PASSES + g + 1) * P)
@@ -252,8 +255,14 @@ def tile_attention_pa_t_kernel(tc, x, rope, qkv_w_words, qkv_w_scales, out_0, ou
                     transpose(i + 1)
                 if i + 2 < CHUNKS:
                     sort(i + 2)
-                banks = project(i)
-                finish_v(i, banks)
+                if i == CHUNKS - 1:
+                    for late_chunk in LATE_V:
+                        finish_v(late_chunk, project(late_chunk, PROJECT_ORDER[:1], xt_pool, "xt"))
+                if i in LATE_V:
+                    banks = project(i, PROJECT_ORDER[1:], acc_pool, "acc")
+                else:
+                    banks = project(i, PROJECT_ORDER, acc_pool, "acc")
+                    finish_v(i, banks)
                 if i == 0:
                     quantise(1)
                 elif i + 1 < CHUNKS:

from contextlib import ExitStack

import concourse.mybir as mybir
from concourse.masks import make_identity

F32 = mybir.dt.float32
BF16 = mybir.dt.bfloat16
I32 = mybir.dt.int32
U32 = mybir.dt.uint32
U8 = mybir.dt.uint8
FP8X4 = mybir.dt.float8_e4m3fn_x4
FP4X4 = mybir.dt.float4_e2m1fn_x4
ALU = mybir.AluOpType

BATCH, TOKENS, K, HEAD = 2, 4096, 1024, 128
COMPONENTS = 3
P = 128
PACK = 4
K_PASS = P * PACK
PASSES = K // K_PASS
TILES = 4
CHUNK = P * TILES
CHUNKS_PER_BATCH = TOKENS // CHUNK
CHUNKS = BATCH * CHUNKS_PER_BATCH
BANK = TILES * HEAD
PAIRS = BANK // 2
WORDS = K // 2
X_BUFFERS = 6
OUT_CHUNKS = 5
PROJECT_ORDER = (2, 0, 1)
VECTOR_SUMS = 3
LATE_V = (4, 9)
SORTED_TILES = 1

FLOPS = 2 * BATCH * TOKENS * K * COMPONENTS * HEAD


def tile_attention_pa_t_kernel(tc, x, rope, qkv_w_words, qkv_w_scales, out_0, out_1, out_2):
    nc = tc.nc

    x_chunks = x.rearrange("b (c p t) k -> (b c) p (t k)", p=P, t=TILES)
    rope_chunks = rope.rearrange("(c p t) o d -> c p (t o d)", p=P, t=TILES)
    out_chunks = [
        o.rearrange("b o (c p t) d -> (b o c) p (t d)", p=P, t=TILES) for o in (out_0, out_1, out_2)
    ]

    with ExitStack() as stack:
        const = stack.enter_context(tc.tile_pool(name="const", bufs=1))
        x_pool = stack.enter_context(tc.tile_pool(name="x", bufs=X_BUFFERS))
        quant = stack.enter_context(tc.tile_pool(name="quant", bufs=2))
        kept_pool = stack.enter_context(tc.tile_pool(name="kept", bufs=len(LATE_V)))
        products = stack.enter_context(tc.tile_pool(name="products", bufs=3))
        rotated_pool = stack.enter_context(tc.tile_pool(name="rotated", bufs=OUT_CHUNKS + 1))
        v_pool = stack.enter_context(tc.tile_pool(name="v", bufs=OUT_CHUNKS))
        xt_pool = stack.enter_context(tc.psum_pool(name="xt", bufs=TILES))
        acc_pool = stack.enter_context(tc.psum_pool(name="acc", bufs=4))

        ident = const.tile([P, P], F32)
        make_identity(nc, ident[:])

        w_words = const.tile([P, PASSES * 2 * COMPONENTS * HEAD], U8, align_bytes=64)
        w_scales = const.tile([P, PASSES * COMPONENTS * HEAD], U8, align_bytes=64)
        nc.vector.memset(w_scales[:].bitcast(I32), 0)

        rope_tiles = [const.tile([P, BANK], BF16, name="rope%d" % c) for c in range(CHUNKS_PER_BATCH)]
        x_tiles = {}

        def load(i, pieces=1):
            x_sb = x_pool.tile([P, TILES * K], BF16)
            width = TILES * K // pieces
            for piece in range(pieces):
                columns = slice(piece * width, (piece + 1) * width)
                nc.sync.dma_start(out=x_sb[:, columns], in_=x_chunks[i][:, columns])
            x_tiles[i] = x_sb

        def load_rope(c):
            nc.sync.dma_start(out=rope_tiles[c][:], in_=rope_chunks[c])

        def load_weights():
            nc.sync.dma_start(
                out=w_words[:].bitcast(I32).rearrange("p (g n) -> p g n", g=PASSES),
                in_=qkv_w_words.bitcast(I32).rearrange("g p n -> p g n"),
            )
            for quadrant in range(4):
                nc.sync.dma_start(
                    out=w_scales[32 * quadrant : 32 * quadrant + 4, :].bitcast(I32).rearrange("r (g n) -> r g n", g=PASSES),
                    in_=qkv_w_scales[:, 4 * quadrant : 4 * quadrant + 4, :].bitcast(I32).rearrange("g r n -> r g n"),
                )

        sorted_tiles = {}
        grouped_tiles = {}
        code_tiles = {}

        def sort(i):
            words = x_tiles[i][:].bitcast(F32)[:, (TILES - SORTED_TILES) * WORDS :]
            by_parity = quant.tile([P, SORTED_TILES * WORDS], F32)
            nc.scalar.copy(
                out=by_parity[:].rearrange("p (h u r) -> p h u r", u=2, r=P),
                in_=words.rearrange("p (h r u) -> p h u r", u=2, r=P),
            )
            sorted_tiles[i] = by_parity

        def transpose(i):
            words = x_tiles[i][:].bitcast(F32)
            by_parity = sorted_tiles.get(i)
            unsorted = TILES if by_parity is None else TILES - SORTED_TILES
            grouped = quant.tile([P, TILES * K], BF16, align_bytes=64)
            grouped_words = grouped[:].bitcast(F32)
            for t in range(TILES):
                xt = xt_pool.tile([P, WORDS], F32, name="xt")
                for g in range(PASSES):
                    for u in range(2):
                        if t < unsorted:
                            first = t * WORDS + g * 2 * P
                            columns = words[:, first + u : first + 2 * P : 2]
                        else:
                            first = (t - unsorted) * WORDS + (2 * g + u) * P
                            columns = by_parity[:, first : first + P]
                        nc.tensor.transpose(xt[:, (2 * g + u) * P : (2 * g + u + 1) * P], columns, ident[:])
                nc.scalar.copy(
                    out=grouped_words[:, t * WORDS : (t + 1) * WORDS].rearrange(
                        "p (g r u) -> p g r u", g=PASSES, u=2
                    ),
                    in_=xt[:].rearrange("p (g u r) -> p g r u", g=PASSES, u=2),
                )
            grouped_tiles[i] = grouped

        def quantise(i, before_last=None):
            pool = kept_pool if i in LATE_V else quant
            codes = pool.tile([P, TILES * PASSES * P], U32, align_bytes=64)
            scales = pool.tile([P, TILES * PASSES * P], U8, align_bytes=64)
            for t in range(TILES):
                columns = slice(t * PASSES * P, (t + 1) * PASSES * P)
                if t == TILES - 1 and before_last is not None:
                    before_last()
                nc.vector.quantize_mx(
                    out=codes[:, columns].bitcast(FP8X4),
                    scales=scales[:, columns],
                    in_=grouped_tiles[i][:, t * K : (t + 1) * K],
                )
            code_tiles[i] = (codes, scales)

        def project(i, components, pool, tag):
            codes, scales = code_tiles[i]
            banks = {}
            for c in components:
                acc = pool.tile([P, BANK], F32, name=tag)
                for t in range(TILES):
                    for g in range(PASSES):
                        tokens = slice((t * PASSES + g) * P, (t * PASSES + g + 1) * P)
                        column = (g * COMPONENTS + c) * HEAD
                        nc.tensor.matmul_mx(
                            out=acc[:, t * HEAD : (t + 1) * HEAD],
                            lhsT=codes[:, tokens].bitcast(FP8X4),
                            lhsT_scale=scales[:, tokens],
                            rhs=w_words[:, 2 * column : 2 * (column + HEAD)].bitcast(FP4X4),
                            rhs_scale=w_scales[:, column : column + HEAD],
                            start=(g == 0),
                            stop=(g == PASSES - 1),
                        )
                banks[c] = acc
            return banks

        pairs = "p (j e) -> p j e"
        HALF = HEAD // 2


        def start_rope(i):
            by_cos = products.tile([P, 2 * BANK], F32)
            by_sin = products.tile([P, 2 * BANK], F32)
            rotated = rotated_pool.tile([P, 2 * BANK], F32)
            return by_cos, by_sin, rotated

        def cos_product(acc, table, by_cos, c):
            cos = table[:].rearrange(pairs, e=2)[:, :, 0:1].to_broadcast([P, PAIRS, 2])
            nc.vector.tensor_tensor(
                out=by_cos[:, c * BANK : (c + 1) * BANK].rearrange(pairs, e=2),
                in0=acc[:].rearrange(pairs, e=2),
                in1=cos,
                op=ALU.mult,
            )

        def sin_product(acc, table, by_sin, c, e, first=0, last=TILES):
            out = by_sin[:, c * BANK : (c + 1) * BANK].rearrange("p (t e j) -> p e t j", t=TILES, e=2)[:, e, first:last, :]
            other = acc[:].rearrange("p (t j e) -> p e t j", t=TILES, e=2)[:, 1 - e, first:last, :]
            sin = table[:].rearrange("p (t j e) -> p e t j", t=TILES, e=2)[:, 1, first:last, :]
            if e == 0:
                nc.vector.scalar_tensor_tensor(out=out, in0=other, scalar=-1.0, in1=sin, op0=ALU.mult, op1=ALU.mult)
            else:
                nc.vector.tensor_tensor(out=out, in0=other, in1=sin, op=ALU.mult)

        def add(engine, by_cos, by_sin, rotated, first, last):
            columns = slice(first * HEAD, last * HEAD)
            engine.tensor_tensor(
                out=rotated[:, columns].rearrange("p (t j e) -> p t j e", j=HALF, e=2),
                in0=by_cos[:, columns].rearrange("p (t j e) -> p t j e", j=HALF, e=2),
                in1=by_sin[:, columns].rearrange("p (t e j) -> p t j e", j=HALF, e=2),
                op=ALU.add,
            )

        held = {}
        late = {}

        def finish_late(i, engine):
            acc, table, by_cos, by_sin, rotated = held[i]
            sin_product(acc, table, by_sin, 1, 1, TILES - 1, TILES)
            add(engine, by_cos, by_sin, rotated, VECTOR_SUMS, 2 * TILES)
            nc.sync.dma_start(out=out_chunks[0][i], in_=rotated[:, 0:BANK])
            nc.sync.dma_start(out=out_chunks[1][i], in_=rotated[:, BANK : 2 * BANK])

        def finish_last(i):
            acc, table, by_cos, by_sin, rotated = held[i]
            sin_product(acc, table, by_sin, 1, 1, TILES - 1, TILES)
            for first in (TILES, TILES + TILES // 2):
                add(nc.vector, by_cos, by_sin, rotated, first, first + TILES // 2)
                columns = slice((first - TILES) * HEAD, (first - TILES // 2) * HEAD)
                nc.sync.dma_start(
                    out=out_chunks[1][i][:, columns], in_=rotated[:, first * HEAD : (first + TILES // 2) * HEAD]
                )

        def finish_v(i, banks):
            v_sb = v_pool.tile([P, BANK], F32)
            nc.scalar.copy(out=v_sb[:], in_=banks[2][:])
            nc.sync.dma_start(out=out_chunks[2][i], in_=v_sb[:])

        def finish(i, banks):
            table = rope_tiles[i % CHUNKS_PER_BATCH]
            by_cos, by_sin, rotated = start_rope(i)
            cos_product(banks[0], table, by_cos, 0)
            sin_product(banks[0], table, by_sin, 0, 0)
            sin_product(banks[0], table, by_sin, 0, 1)
            cos_product(banks[1], table, by_cos, 1)
            sin_product(banks[1], table, by_sin, 1, 0)
            sin_product(banks[1], table, by_sin, 1, 1, 0, TILES - 1)
            held[i] = (banks[1], table, by_cos, by_sin, rotated)
            late[i] = lambda: finish_late(i, nc.gpsimd)
            if i < CHUNKS - 1:
                add(nc.vector, by_cos, by_sin, rotated, 0, VECTOR_SUMS)
            else:
                add(nc.vector, by_cos, by_sin, rotated, 0, TILES)
                nc.sync.dma_start(out=out_chunks[0][i], in_=rotated[:, 0:BANK])

        with tc.manual_schedule():
            load(0, pieces=TILES)
            load(1, pieces=TILES)
            load_weights()
            load_rope(0)
            for i in range(2, X_BUFFERS):
                load(i)
                load_rope(i - 1)
            transpose(0)
            quantise(0)
            for i in range(CHUNKS):
                if i + 1 < CHUNKS:
                    transpose(i + 1)
                if i + 2 < CHUNKS:
                    sort(i + 2)
                if i == CHUNKS - 1:
                    for late_chunk in LATE_V:
                        finish_v(late_chunk, project(late_chunk, PROJECT_ORDER[:1], xt_pool, "xt"))
                if i in LATE_V:
                    banks = project(i, PROJECT_ORDER[1:], acc_pool, "acc")
                else:
                    banks = project(i, PROJECT_ORDER, acc_pool, "acc")
                    finish_v(i, banks)
                if i == 0:
                    quantise(1)
                elif i + 1 < CHUNKS:
                    quantise(i + 1, before_last=late[i - 1])
                else:
                    late[i - 1]()
                finish(i, banks)
                if i + X_BUFFERS < CHUNKS:
                    load(i + X_BUFFERS)
                if i + X_BUFFERS - 1 < CHUNKS_PER_BATCH:
                    load_rope(i + X_BUFFERS - 1)
            finish_last(CHUNKS - 1)
